import numpy as np
import ml_dtypes


def mxq(x, axis, fmt="e4m3"):
    dtype, down = {"e4m3": (ml_dtypes.float8_e4m3fn, 7), "e5m2": (ml_dtypes.float8_e5m2, 14)}[fmt]
    v = np.moveaxis(np.asarray(x, np.float32).astype(ml_dtypes.bfloat16).astype(np.float64), axis, -1)
    blocks = v.reshape(v.shape[:-1] + (-1, 32))
    amax = np.abs(blocks).max(-1, keepdims=True)
    byte = np.maximum(np.where(amax > 0, np.frexp(amax)[1] - 1 + 127, 0) - down, 1)
    scale = np.exp2(byte - 127.0)
    codes = (blocks / scale).astype(np.float32).astype(dtype).astype(np.float64)
    return np.moveaxis((codes * scale).reshape(v.shape), -1, axis)


WIDE = False


def mx_kscale(k):
    if not WIDE:
        return np.ones(k)
    levels = np.array([10, -10, 5, -5, 0])
    if k % 512:
        return np.exp2(np.random.permutation(np.resize(levels, k // 32))).repeat(32)
    a = np.empty((k // 512, 16))
    for p in range(k // 512):
        a[p, :8] = np.random.permutation(np.resize(levels, 8))
        for g in range(8):
            far = levels[np.abs(levels - a[p, g]) >= 10]
            a[p, g + 8] = far[np.random.randint(len(far))]
    return np.exp2(a.ravel()).repeat(32)


BF16 = ml_dtypes.bfloat16


def bf(x):
    return np.asarray(x, np.float32).astype(BF16)


def f64(x):
    return np.asarray(x).astype(np.float64)


B, S, H, NH, FF = 8, 512, 512, 4, 3072
HD = H // NH
EPS = 1e-7


def layer_norm(x, g, b):
    m = x.mean(-1, keepdims=True)
    v = ((x - m) ** 2).mean(-1, keepdims=True)
    return (x - m) / np.sqrt(v + EPS) * g + b


def heads(t):
    return t.reshape(B, S, NH, HD).transpose(0, 2, 1, 3)


def setup_inputs():
    s = mx_kscale(H)
    r = np.random.standard_normal
    return {"x": bf(r((B, S, H))), "pos_emb": bf(r((S, H)) * 0.5),
            "emb_ln_g": bf((1.0 + 0.1 * r(H)) * s), "emb_ln_b": bf(0.1 * r(H) * s),
            "Wq": bf(r((H, H)) * 1.5 / np.sqrt(H) / s[:, None]),
            "Wk": bf(r((H, H)) * 1.5 / np.sqrt(H) / s[:, None]),
            "Wv": bf(r((H, H)) * 2.0 / np.sqrt(H) / s[:, None]),
            "q_bias": bf(r(H) * 0.3), "v_bias": bf(r(H) * 0.3)}


def reference(x, pos_emb, emb_ln_g, emb_ln_b, Wq, Wk, Wv, q_bias, v_bias):
    h = layer_norm(f64(x) + f64(pos_emb), f64(emb_ln_g), f64(emb_ln_b))
    hq = mxq(h, 2, "e4m3")
    q = heads((hq @ mxq(f64(Wq), 0, "e4m3")) + f64(q_bias))
    k = heads(hq @ mxq(f64(Wk), 0, "e4m3"))
    v = heads((hq @ mxq(f64(Wv), 0, "e4m3")) + f64(v_bias))
    return q / np.sqrt(HD), k, v

@@ -1,0 +1,272 @@
+from contextlib import ExitStack
+import math
+
+import concourse.mybir as mybir
+from concourse.masks import make_identity
+
+F32 = mybir.dt.float32
+BF16 = mybir.dt.bfloat16
+U32 = mybir.dt.uint32
+U8 = mybir.dt.uint8
+FP8X4 = mybir.dt.float8_e4m3fn_x4
+ALU = mybir.AluOpType
+ACT = mybir.ActivationFunctionType
+
+P = 128
+PACK = 4
+B, S, H, NH, HD = 8, 512, 512, 4, 128
+ROW_TILES = S // P
+EPS = 1e-7
+Q_SCALE = 1.0 / math.sqrt(HD)
+
+Q, K, V = 0, 1, 2
+
+FLOPS = 2 * B * S * H * 3 * H
+
+
+def tile_disentangledattention_pa_t_kernel(
+    tc, x, pos_emb, emb_ln_g, emb_ln_b, Wq, Wk, Wv, q_bias, v_bias, out_0, out_1, out_2
+):
+    nc = tc.nc
+    with ExitStack() as ctx:
+        ctx.enter_context(tc.manual_schedule())
+        const = ctx.enter_context(tc.tile_pool(name="const", bufs=1))
+        xs = ctx.enter_context(tc.tile_pool(name="xs", bufs=B))
+        work = ctx.enter_context(tc.tile_pool(name="work", bufs=2))
+        small = ctx.enter_context(tc.tile_pool(name="small", bufs=3))
+        outs = ctx.enter_context(tc.tile_pool(name="outs", bufs=3))
+        psum_t = ctx.enter_context(tc.psum_pool(name="psum_t", bufs=3))
+        psum_acc = ctx.enter_context(tc.psum_pool(name="psum_acc", bufs=5))
+
+        x_sb, u, stats, mean_var, std, neg_mean, rstd = {}, {}, {}, {}, {}, {}, {}
+        z, z_t, h_t, grouped, h_codes, h_scales = {}, {}, {}, {}, {}, {}
+
+        def live(b):
+            return 0 <= b < B
+
+        def load_x(b):
+            x_sb[b] = xs.tile([P, ROW_TILES, H], BF16, name="x_b")
+            nc.sync.dma_start(out=x_sb[b][:], in_=x[b].rearrange("(p j) h -> p j h", j=ROW_TILES))
+
+        def regroup(copy, dst, src):
+            copy(
+                out=dst.rearrange("p (c i) t -> p c t i", i=4),
+                in_=src.rearrange("p t (c i) -> p c t i", i=4),
+            )
+
+        def elementwise_engine(b):
+            return nc.vector if b == 0 else nc.gpsimd
+
+        def add_pos(b):
+            u[b] = work.tile([P, ROW_TILES, H], F32, name="u", bufs=3)
+            elementwise_engine(b).tensor_tensor(out=u[b][:], in0=x_sb[b][:], in1=pos_sb[:], op=ALU.add)
+            stats[b] = small.tile([P, ROW_TILES, 6], F32, name="stats")
+            mean_var[b] = small.tile([P, ROW_TILES, 2], F32, name="mean_var")
+
+        def row_stats(b, j):
+            nc.vector.bn_stats(out=stats[b][:, j, :], in_=u[b][:, j, :])
+            nc.vector.bn_aggr(out=mean_var[b][:, j, :], in_=stats[b][:, j, :])
+
+        def row_std(b):
+            std[b] = small.tile([P, ROW_TILES], F32, name="std")
+            nc.scalar.activation(
+                out=std[b][:], in_=mean_var[b][:, :, 1], func=ACT.Sqrt, bias=EPS, scale=1.0
+            )
+
+        def row_factors(b):
+            rstd[b] = small.tile([P, ROW_TILES], F32, name="rstd")
+            nc.vector.reciprocal(out=rstd[b][:], in_=std[b][:])
+            neg_mean[b] = small.tile([P, ROW_TILES], F32, name="neg_mean")
+            nc.vector.tensor_scalar_mul(out=neg_mean[b][:], in0=mean_var[b][:, :, 0], scalar1=-1.0)
+
+        def normalise(b):
+            z[b] = work.tile([P, ROW_TILES, PACK, P], F32, name="z")
+            h_t[b] = work.tile([P, PACK, S], BF16, name="h_t")
+            for j in range(ROW_TILES):
+                engine = elementwise_engine(b) if j % 2 == 0 else nc.vector
+                engine.tensor_scalar(
+                    out=z[b][:, j, :, :].rearrange("p t (c i) -> p c t i", i=4),
+                    in0=u[b][:, j, :].rearrange("p (c i t) -> p c t i", i=4, t=PACK),
+                    scalar1=neg_mean[b][:, j : j + 1],
+                    scalar2=rstd[b][:, j : j + 1],
+                    op0=ALU.add,
+                    op1=ALU.mult,
+                )
+
+        def transpose(b, t):
+            z_t[b, t] = psum_t.tile([P, S], F32, name="z_t")
+            for j in range(ROW_TILES):
+                nc.tensor.transpose(
+                    z_t[b, t][:, j * P : (j + 1) * P], z[b][:, j, t, :], ident_f32[:]
+                )
+
+        def gain_bias(b, t):
+            nc.scalar.activation(
+                out=h_t[b][:, t, :],
+                in_=z_t[b, t][:],
+                func=ACT.Identity,
+                scale=gb_col[:, t : t + 1],
+                bias=gb_col[:, PACK + t : PACK + t + 1],
+            )
+
+        def regroup_h(b):
+            grouped[b] = work.tile([P, S, PACK], BF16, name="grouped", align_bytes=64)
+            regroup(nc.scalar.copy if b < B - 2 else nc.vector.tensor_copy, grouped[b][:], h_t[b][:])
+
+        def quantise_h(b):
+            h_codes[b] = work.tile([P, S], U32, name="h_codes", align_bytes=64)
+            h_scales[b] = work.tile([P, S], U8, name="h_scales", align_bytes=64)
+            nc.vector.quantize_mx(
+                out=h_codes[b][:].bitcast(FP8X4),
+                scales=h_scales[b][:],
+                in_=grouped[b][:].rearrange("p r t -> p (r t)"),
+            )
+
+        def project(b, i, j, o_sb):
+            rows = slice(j * P, (j + 1) * P)
+            acc = psum_acc.tile([P, H], F32, name="acc", tag="acc")
+            nc.tensor.matmul_mx(
+                out=acc[:],
+                lhsT=h_codes[b][:, rows].bitcast(FP8X4),
+                lhsT_scale=h_scales[b][:, rows],
+                rhs=w_codes[i][:].bitcast(FP8X4),
+                rhs_scale=w_scales[i][:],
+                start=True,
+                stop=True,
+            )
+            by_head = acc[:].rearrange("p (n d) -> p n d", n=NH)
+            if i == Q:
+                nc.vector.scalar_tensor_tensor(
+                    out=o_sb[:, :, j, :],
+                    in0=by_head,
+                    scalar=Q_SCALE,
+                    in1=qb_scaled[:].rearrange("p (n d) -> p n d", n=NH),
+                    op0=ALU.mult,
+                    op1=ALU.add,
+                )
+            elif i == K:
+                nc.scalar.copy(out=o_sb[:, :, j, :], in_=by_head)
+            else:
+                nc.vector.tensor_tensor(
+                    out=o_sb[:, :, j, :],
+                    in0=by_head,
+                    in1=vb_bc[:].rearrange("p (n d) -> p n d", n=NH),
+                    op=ALU.add,
+                )
+
+        def store(b, o_sb, o_dram):
+            nc.sync.dma_start(
+                out=o_dram[b].rearrange("n (p j) d -> p n (j d)", j=ROW_TILES),
+                in_=o_sb[:].rearrange("p n j d -> p n (j d)"),
+            )
+
+        load_x(0)
+        pos_sb = const.tile([P, ROW_TILES, H], BF16)
+        nc.sync.dma_start(out=pos_sb[:], in_=pos_emb.rearrange("(p j) h -> p j h", j=ROW_TILES))
+        g_raw = const.tile([P, PACK], BF16)
+        nc.sync.dma_start(out=g_raw[:], in_=emb_ln_g.rearrange("(p t) -> p t", t=PACK))
+        b_raw = const.tile([P, PACK], BF16)
+        nc.sync.dma_start(out=b_raw[:], in_=emb_ln_b.rearrange("(p t) -> p t", t=PACK))
+        load_x(1)
+        w_raw, w_grouped, w_codes, w_scales = [], [], [], []
+        for i, w in enumerate((Wq, Wk, Wv)):
+            raw = const.tile([P, PACK, H], BF16, name="w_raw%d" % i)
+            nc.sync.dma_start(out=raw[:], in_=w.rearrange("(p t) n -> p t n", t=PACK))
+            w_raw.append(raw)
+            g_w = const.tile([P, H, PACK], BF16, name="w_grouped%d" % i, align_bytes=64)
+            w_grouped.append(g_w)
+            codes = const.tile([P, H], U32, name="w_codes%d" % i, align_bytes=64)
+            w_codes.append(codes)
+            scales = const.tile([P, H], U8, name="w_scales%d" % i, align_bytes=64)
+            w_scales.append(scales)
+        load_x(2)
+        qb_bc = const.tile([P, H], BF16)
+        nc.sync.dma_start(out=qb_bc[:], in_=q_bias.partition_broadcast(P))
+        vb_bc = const.tile([P, H], BF16)
+        nc.sync.dma_start(out=vb_bc[:], in_=v_bias.partition_broadcast(P))
+        for b in range(3, B):
+            load_x(b)
+
+        ident_f32 = const.tile([P, P], F32)
+        make_identity(nc, ident_f32[:])
+        one = const.tile([P, 1], F32)
+        nc.vector.memset(one[:], 1.0)
+        warm = const.tile([P, 1], F32)
+        nc.scalar.activation(out=warm[:], in_=one[:], func=ACT.Sqrt)
+        gb_col = const.tile([P, 2 * PACK], F32)
+        qb_scaled = const.tile([P, H], F32)
+
+        for step in range(-4, B):
+            o_sb = []
+            if live(step):
+                for i in range(3):
+                    o_i = outs.tile([P, NH, ROW_TILES, HD], F32, name="o%d" % i)
+                    o_sb.append(o_i)
+            if live(step + 2):
+                normalise(step + 2)
+            if live(step + 4):
+                add_pos(step + 4)
+            if step == -3:
+                regroup(nc.scalar.copy, w_grouped[Q][:], w_raw[Q][:])
+
+            if live(step):
+                project(step, Q, 0, o_sb[Q])
+                project(step, Q, 1, o_sb[Q])
+                project(step, K, 0, o_sb[K])
+            if live(step + 1):
+                regroup_h(step + 1)
+            if live(step + 3):
+                row_stats(step + 3, 0)
+                row_stats(step + 3, 1)
+            if live(step):
+                project(step, Q, 2, o_sb[Q])
+                project(step, Q, 3, o_sb[Q])
+                project(step, K, 1, o_sb[K])
+                store(step, o_sb[Q], out_0)
+            if live(step + 2):
+                transpose(step + 2, 0)
+                transpose(step + 2, 1)
+                transpose(step + 2, 2)
+            if live(step + 3):
+                row_stats(step + 3, 2)
+                row_stats(step + 3, 3)
+            if step == -3:
+                nc.vector.tensor_copy(out=gb_col[:, 0:PACK], in_=g_raw[:])
+                nc.vector.tensor_copy(out=gb_col[:, PACK : 2 * PACK], in_=b_raw[:])
+            if live(step + 2):
+                gain_bias(step + 2, 0)
+            if live(step + 3):
+                row_std(step + 3)
+            if step == -3:
+                regroup(nc.scalar.copy, w_grouped[K][:], w_raw[K][:])
+                regroup(nc.scalar.copy, w_grouped[V][:], w_raw[V][:])
+            if step == -2:
+                for i in range(3):
+                    nc.vector.quantize_mx(
+                        out=w_codes[i][:].bitcast(FP8X4),
+                        scales=w_scales[i][:],
+                        in_=w_grouped[i][:].rearrange("p n t -> p (n t)"),
+                    )
+                nc.vector.tensor_scalar_mul(out=qb_scaled[:], in0=qb_bc[:], scalar1=Q_SCALE)
+            if live(step + 1):
+                quantise_h(step + 1)
+            if live(step + 2):
+                gain_bias(step + 2, 1)
+            if live(step):
+                project(step, V, 0, o_sb[V])
+                project(step, V, 1, o_sb[V])
+                project(step, K, 2, o_sb[K])
+            if live(step + 3):
+                row_factors(step + 3)
+            if live(step + 2):
+                transpose(step + 2, 3)
+                gain_bias(step + 2, 2)
+            if live(step):
+                project(step, V, 2, o_sb[V])
+                project(step, V, 3, o_sb[V])
+                project(step, K, 3, o_sb[K])
+            if live(step + 2):
+                gain_bias(step + 2, 3)
+            if live(step):
+                store(step, o_sb[K], out_1)
+                store(step, o_sb[V], out_2)

@@ -31,62 +31,88 @@ def tile_disentangledattention_pa_t_kernel(
     with ExitStack() as ctx:
         ctx.enter_context(tc.manual_schedule())
         const = ctx.enter_context(tc.tile_pool(name="const", bufs=1))
-        xs = ctx.enter_context(tc.tile_pool(name="xs", bufs=B))
+        xs = ctx.enter_context(tc.tile_pool(name="xs", bufs=6))
         work = ctx.enter_context(tc.tile_pool(name="work", bufs=2))
-        small = ctx.enter_context(tc.tile_pool(name="small", bufs=3))
+        small = ctx.enter_context(tc.tile_pool(name="small", bufs=6))
         outs = ctx.enter_context(tc.tile_pool(name="outs", bufs=3))
         psum_t = ctx.enter_context(tc.psum_pool(name="psum_t", bufs=3))
-        psum_acc = ctx.enter_context(tc.psum_pool(name="psum_acc", bufs=5))
+        psum_qv = ctx.enter_context(tc.psum_pool(name="psum_qv", bufs=3))
+        psum_k = ctx.enter_context(tc.psum_pool(name="psum_k", bufs=2))
 
-        x_sb, u, stats, mean_var, std, neg_mean, rstd = {}, {}, {}, {}, {}, {}, {}
-        z, z_t, h_t, grouped, h_codes, h_scales = {}, {}, {}, {}, {}, {}
+        x_sb, u, total, square, std, neg_mean, rstd, neg_shift = {}, {}, {}, {}, {}, {}, {}, {}
+        z, z_t, h_t, grouped, h_codes, h_scales, acc_of, o_sb = {}, {}, {}, {}, {}, {}, {}, {}
 
         def live(b):
             return 0 <= b < B
 
-        def load_x(b):
-            x_sb[b] = xs.tile([P, ROW_TILES, H], BF16, name="x_b")
-            nc.sync.dma_start(out=x_sb[b][:], in_=x[b].rearrange("(p j) h -> p j h", j=ROW_TILES))
-
-        def regroup(copy, dst, src):
-            copy(
-                out=dst.rearrange("p (c i) t -> p c t i", i=4),
-                in_=src.rearrange("p t (c i) -> p c t i", i=4),
+        def load_rows(dst, src, j0, j1):
+            nc.sync.dma_start(
+                out=dst[:, j0:j1, :], in_=src.rearrange("(p j) h -> p j h", j=ROW_TILES)[:, j0:j1, :]
             )
 
-        def elementwise_engine(b):
-            return nc.vector if b == 0 else nc.gpsimd
+        def new_x(b):
+            x_sb[b] = xs.tile([P, ROW_TILES, H], BF16, name="x_b")
 
-        def add_pos(b):
-            u[b] = work.tile([P, ROW_TILES, H], F32, name="u", bufs=3)
-            elementwise_engine(b).tensor_tensor(out=u[b][:], in0=x_sb[b][:], in1=pos_sb[:], op=ALU.add)
-            stats[b] = small.tile([P, ROW_TILES, 6], F32, name="stats")
-            mean_var[b] = small.tile([P, ROW_TILES, 2], F32, name="mean_var")
+        def add_pos(b, j):
+            if j == 0:
+                u[b] = work.tile([P, ROW_TILES, H], F32, name="u", bufs=5)
+                total[b] = small.tile([P, ROW_TILES], F32, name="total")
+            nc.vector.scalar_tensor_tensor(
+                out=u[b][:, j, :],
+                in0=x_sb[b][:, j, :],
+                scalar=1.0,
+                in1=pos_sb[:, j, :],
+                op0=ALU.mult,
+                op1=ALU.add,
+                accum_out=total[b][:, j : j + 1],
+            )
 
-        def row_stats(b, j):
-            nc.vector.bn_stats(out=stats[b][:, j, :], in_=u[b][:, j, :])
-            nc.vector.bn_aggr(out=mean_var[b][:, j, :], in_=stats[b][:, j, :])
+        def square_dev(b, j):
+            if j == 0:
+                square[b] = small.tile([P, ROW_TILES], F32, name="square")
+            dev = work.tile([P, H], BF16, name="dev")
+            nc.scalar.activation(
+                out=dev[:],
+                in_=u[b][:, j, :],
+                func=ACT.Square,
+                scale=-float(H),
+                bias=total[b][:, j : j + 1],
+                accum_out=square[b][:, j : j + 1],
+            )
 
         def row_std(b):
             std[b] = small.tile([P, ROW_TILES], F32, name="std")
             nc.scalar.activation(
-                out=std[b][:], in_=mean_var[b][:, :, 1], func=ACT.Sqrt, bias=EPS, scale=1.0
+                out=std[b][:], in_=square[b][:], func=ACT.Sqrt, bias=EPS, scale=1.0 / float(H) ** 3
             )
+
+        def row_mean(b):
+            neg_mean[b] = small.tile([P, ROW_TILES], F32, name="neg_mean")
+            nc.vector.tensor_scalar_mul(out=neg_mean[b][:], in0=total[b][:], scalar1=-1.0 / H)
 
         def row_factors(b):
             rstd[b] = small.tile([P, ROW_TILES], F32, name="rstd")
             nc.vector.reciprocal(out=rstd[b][:], in_=std[b][:])
-            neg_mean[b] = small.tile([P, ROW_TILES], F32, name="neg_mean")
-            nc.vector.tensor_scalar_mul(out=neg_mean[b][:], in0=mean_var[b][:, :, 0], scalar1=-1.0)
+            neg_shift[b] = small.tile([P, ROW_TILES], F32, name="neg_shift")
+            nc.vector.tensor_tensor(out=neg_shift[b][:], in0=neg_mean[b][:], in1=rstd[b][:], op=ALU.mult)
 
-        def normalise(b):
-            z[b] = work.tile([P, ROW_TILES, PACK, P], F32, name="z")
-            h_t[b] = work.tile([P, PACK, S], BF16, name="h_t")
-            for j in range(ROW_TILES):
-                engine = elementwise_engine(b) if j % 2 == 0 else nc.vector
+        def normalise(b, j, engine):
+            if j == 0:
+                z[b] = work.tile([P, ROW_TILES, PACK, P], F32, name="z", bufs=3)
+            z_j = z[b][:, j, :, :].rearrange("p t (c i) -> p c t i", i=4)
+            u_j = u[b][:, j, :].rearrange("p (c i t) -> p c t i", i=4, t=PACK)
+            if engine is nc.scalar:
+                nc.scalar.activation(
+                    out=z_j,
+                    in_=u_j,
+                    func=ACT.Identity,
+                    scale=rstd[b][:, j : j + 1],
+                    bias=neg_shift[b][:, j : j + 1],
+                )
+            else:
                 engine.tensor_scalar(
-                    out=z[b][:, j, :, :].rearrange("p t (c i) -> p c t i", i=4),
-                    in0=u[b][:, j, :].rearrange("p (c i t) -> p c t i", i=4, t=PACK),
+                    out=z_j,
+                    in0=u_j,
                     scalar1=neg_mean[b][:, j : j + 1],
                     scalar2=rstd[b][:, j : j + 1],
                     op0=ALU.add,
@@ -96,35 +122,53 @@ def tile_disentangledattention_pa_t_kernel(
         def transpose(b, t):
             z_t[b, t] = psum_t.tile([P, S], F32, name="z_t")
             for j in range(ROW_TILES):
-                nc.tensor.transpose(
-                    z_t[b, t][:, j * P : (j + 1) * P], z[b][:, j, t, :], ident_f32[:]
-                )
+                nc.tensor.transpose(z_t[b, t][:, j * P : (j + 1) * P], z[b][:, j, t, :], ident[:])
 
         def gain_bias(b, t):
+            if t == 0:
+                h_t[b] = work.tile([P, PACK, S], BF16, name="h_t")
             nc.scalar.activation(
                 out=h_t[b][:, t, :],
                 in_=z_t[b, t][:],
                 func=ACT.Identity,
-                scale=gb_col[:, t : t + 1],
-                bias=gb_col[:, PACK + t : PACK + t + 1],
+                scale=gain[:, t : t + 1],
+                bias=shift[:, t : t + 1],
             )
 
-        def regroup_h(b):
+        def regroup(copy, dst, src):
+            if copy is gpsimd_copy:
+                copy(out=dst, in_=src.rearrange("p t c -> p c t"))
+                return
+            copy(
+                out=dst.rearrange("p (c i) t -> p c t i", i=4),
+                in_=src.rearrange("p t (c i) -> p c t i", i=4),
+            )
+
+        def gpsimd_copy(out, in_):
+            nc.gpsimd.tensor_scalar(out=out, in0=in_, scalar1=1.0, scalar2=0.0, op0=ALU.mult, op1=ALU.add)
+
+        def regroup_h(b, copy):
             grouped[b] = work.tile([P, S, PACK], BF16, name="grouped", align_bytes=64)
-            regroup(nc.scalar.copy if b < B - 2 else nc.vector.tensor_copy, grouped[b][:], h_t[b][:])
+            regroup(copy, grouped[b][:], h_t[b][:])
+
+        def quantise(codes, scales, src):
+            nc.vector.quantize_mx(
+                out=codes[:].bitcast(FP8X4), scales=scales[:], in_=src[:].rearrange("p r t -> p (r t)")
+            )
 
         def quantise_h(b):
             h_codes[b] = work.tile([P, S], U32, name="h_codes", align_bytes=64)
             h_scales[b] = work.tile([P, S], U8, name="h_scales", align_bytes=64)
-            nc.vector.quantize_mx(
-                out=h_codes[b][:].bitcast(FP8X4),
-                scales=h_scales[b][:],
-                in_=grouped[b][:].rearrange("p r t -> p (r t)"),
-            )
+            quantise(h_codes[b], h_scales[b], grouped[b])
 
-        def project(b, i, j, o_sb):
+        def multiply(b, i, j):
+            if j == 0:
+                o_sb[b, i] = outs.tile([P, NH, ROW_TILES, HD], F32, name="o%d" % i)
             rows = slice(j * P, (j + 1) * P)
-            acc = psum_acc.tile([P, H], F32, name="acc", tag="acc")
+            if i == K:
+                acc = psum_k.tile([P, H], F32, name="acc_k")
+            else:
+                acc = psum_qv.tile([P, H], F32, name="acc_qv")
             nc.tensor.matmul_mx(
                 out=acc[:],
                 lhsT=h_codes[b][:, rows].bitcast(FP8X4),
@@ -134,40 +178,37 @@ def tile_disentangledattention_pa_t_kernel(
                 start=True,
                 stop=True,
             )
-            by_head = acc[:].rearrange("p (n d) -> p n d", n=NH)
+            acc_of[b, i, j] = acc
+
+        def evacuate(b, i, j):
+            by_head = acc_of[b, i, j][:].rearrange("p (n d) -> p n d", n=NH)
+            o_j = o_sb[b, i][:, :, j, :]
             if i == Q:
                 nc.vector.scalar_tensor_tensor(
-                    out=o_sb[:, :, j, :],
-                    in0=by_head,
-                    scalar=Q_SCALE,
-                    in1=qb_scaled[:].rearrange("p (n d) -> p n d", n=NH),
-                    op0=ALU.mult,
-                    op1=ALU.add,
+                    out=o_j, in0=by_head, scalar=Q_SCALE, in1=q_add[:], op0=ALU.mult, op1=ALU.add
                 )
             elif i == K:
-                nc.scalar.copy(out=o_sb[:, :, j, :], in_=by_head)
+                nc.scalar.copy(out=o_j, in_=by_head)
             else:
-                nc.vector.tensor_tensor(
-                    out=o_sb[:, :, j, :],
-                    in0=by_head,
-                    in1=vb_bc[:].rearrange("p (n d) -> p n d", n=NH),
-                    op=ALU.add,
-                )
+                nc.vector.tensor_tensor(out=o_j, in0=by_head, in1=v_add[:], op=ALU.add)
 
-        def store(b, o_sb, o_dram):
+        def store(b, i):
             nc.sync.dma_start(
-                out=o_dram[b].rearrange("n (p j) d -> p n (j d)", j=ROW_TILES),
-                in_=o_sb[:].rearrange("p n j d -> p n (j d)"),
+                out=(out_0, out_1, out_2)[i][b].rearrange("n (p j) d -> p n (j d)", j=ROW_TILES),
+                in_=o_sb[b, i][:].rearrange("p n j d -> p n (j d)"),
             )
 
-        load_x(0)
         pos_sb = const.tile([P, ROW_TILES, H], BF16)
-        nc.sync.dma_start(out=pos_sb[:], in_=pos_emb.rearrange("(p j) h -> p j h", j=ROW_TILES))
-        g_raw = const.tile([P, PACK], BF16)
-        nc.sync.dma_start(out=g_raw[:], in_=emb_ln_g.rearrange("(p t) -> p t", t=PACK))
-        b_raw = const.tile([P, PACK], BF16)
-        nc.sync.dma_start(out=b_raw[:], in_=emb_ln_b.rearrange("(p t) -> p t", t=PACK))
-        load_x(1)
+        new_x(0)
+        for j in (0, 2):
+            load_rows(x_sb[0], x[0], j, j + 2)
+            load_rows(pos_sb, pos_emb, j, j + 2)
+        new_x(1)
+        load_rows(x_sb[1], x[1], 0, ROW_TILES)
+        gain_raw = const.tile([P, PACK], BF16)
+        nc.sync.dma_start(out=gain_raw[:], in_=emb_ln_g.rearrange("(p t) -> p t", t=PACK))
+        shift_raw = const.tile([P, PACK], BF16)
+        nc.sync.dma_start(out=shift_raw[:], in_=emb_ln_b.rearrange("(p t) -> p t", t=PACK))
         w_raw, w_grouped, w_codes, w_scales = [], [], [], []
         for i, w in enumerate((Wq, Wk, Wv)):
             raw = const.tile([P, PACK, H], BF16, name="w_raw%d" % i)
@@ -179,94 +220,157 @@ def tile_disentangledattention_pa_t_kernel(
             w_codes.append(codes)
             scales = const.tile([P, H], U8, name="w_scales%d" % i, align_bytes=64)
             w_scales.append(scales)
-        load_x(2)
-        qb_bc = const.tile([P, H], BF16)
-        nc.sync.dma_start(out=qb_bc[:], in_=q_bias.partition_broadcast(P))
-        vb_bc = const.tile([P, H], BF16)
-        nc.sync.dma_start(out=vb_bc[:], in_=v_bias.partition_broadcast(P))
-        for b in range(3, B):
-            load_x(b)
+        bias_rows = []
+        for i, bias in enumerate((q_bias, v_bias)):
+            row = const.tile([P, H], BF16, name="bias_row%d" % i)
+            nc.gpsimd.memset(row[:], 0.0)
+            nc.sync.dma_start(out=row[0:1, :], in_=bias.unsqueeze(0))
+            bias_rows.append(row)
+        for b in range(2, B):
+            new_x(b)
+            load_rows(x_sb[b], x[b], 0, ROW_TILES)
 
-        ident_f32 = const.tile([P, P], F32)
-        make_identity(nc, ident_f32[:])
+        ident = const.tile([P, P], F32)
+        make_identity(nc, ident[:])
+        ones = const.tile([P, P], BF16)
+        nc.gpsimd.memset(ones[:], 1.0)
         one = const.tile([P, 1], F32)
-        nc.vector.memset(one[:], 1.0)
+        nc.gpsimd.memset(one[:], 1.0)
         warm = const.tile([P, 1], F32)
         nc.scalar.activation(out=warm[:], in_=one[:], func=ACT.Sqrt)
-        gb_col = const.tile([P, 2 * PACK], F32)
-        qb_scaled = const.tile([P, H], F32)
+        gain = const.tile([P, PACK], F32)
+        shift = const.tile([P, PACK], F32)
+        q_add = const.tile([P, NH, HD], F32)
+        v_add = const.tile([P, NH, HD], F32)
 
-        for step in range(-4, B):
-            o_sb = []
-            if live(step):
-                for i in range(3):
-                    o_i = outs.tile([P, NH, ROW_TILES, HD], F32, name="o%d" % i)
-                    o_sb.append(o_i)
-            if live(step + 2):
-                normalise(step + 2)
-            if live(step + 4):
-                add_pos(step + 4)
-            if step == -3:
-                regroup(nc.scalar.copy, w_grouped[Q][:], w_raw[Q][:])
+        def spread_bias(row, dst, scale):
+            bank = psum_k.tile([P, H], F32, name="acc_k")
+            nc.tensor.matmul(bank[:], lhsT=ones[:], rhs=row[:], start=True, stop=True)
+            nc.scalar.activation(
+                out=dst[:].rearrange("p n d -> p (n d)"), in_=bank[:], func=ACT.Copy, scale=scale
+            )
 
-            if live(step):
-                project(step, Q, 0, o_sb[Q])
-                project(step, Q, 1, o_sb[Q])
-                project(step, K, 0, o_sb[K])
-            if live(step + 1):
-                regroup_h(step + 1)
-            if live(step + 3):
-                row_stats(step + 3, 0)
-                row_stats(step + 3, 1)
-            if live(step):
-                project(step, Q, 2, o_sb[Q])
-                project(step, Q, 3, o_sb[Q])
-                project(step, K, 1, o_sb[K])
-                store(step, o_sb[Q], out_0)
-            if live(step + 2):
-                transpose(step + 2, 0)
-                transpose(step + 2, 1)
-                transpose(step + 2, 2)
-            if live(step + 3):
-                row_stats(step + 3, 2)
-                row_stats(step + 3, 3)
-            if step == -3:
-                nc.vector.tensor_copy(out=gb_col[:, 0:PACK], in_=g_raw[:])
-                nc.vector.tensor_copy(out=gb_col[:, PACK : 2 * PACK], in_=b_raw[:])
-            if live(step + 2):
-                gain_bias(step + 2, 0)
-            if live(step + 3):
-                row_std(step + 3)
-            if step == -3:
-                regroup(nc.scalar.copy, w_grouped[K][:], w_raw[K][:])
-                regroup(nc.scalar.copy, w_grouped[V][:], w_raw[V][:])
-            if step == -2:
-                for i in range(3):
-                    nc.vector.quantize_mx(
-                        out=w_codes[i][:].bitcast(FP8X4),
-                        scales=w_scales[i][:],
-                        in_=w_grouped[i][:].rearrange("p n t -> p (n t)"),
-                    )
-                nc.vector.tensor_scalar_mul(out=qb_scaled[:], in0=qb_bc[:], scalar1=Q_SCALE)
-            if live(step + 1):
+        def weight(i, copy):
+            regroup(copy, w_grouped[i][:], w_raw[i][:])
+
+        def sums(b, j):
+            add_pos(b, j)
+            square_dev(b, j)
+
+        for j in range(ROW_TILES):
+            sums(0, j)
+        row_std(0)
+        row_mean(0)
+        add_pos(1, 0)
+        add_pos(1, 1)
+        nc.vector.tensor_copy(out=gain[:], in_=gain_raw[:])
+        nc.vector.tensor_copy(out=shift[:], in_=shift_raw[:])
+        row_factors(0)
+        for j in range(ROW_TILES):
+            normalise(0, j, nc.vector if j < 2 else nc.scalar)
+        for t in range(PACK):
+            transpose(0, t)
+            gain_bias(0, t)
+        add_pos(1, 2)
+        add_pos(1, 3)
+        row_mean(1)
+        weight(Q, nc.vector.tensor_copy)
+        for j in range(ROW_TILES):
+            square_dev(1, j)
+        row_std(1)
+        add_pos(2, 0)
+        quantise(w_codes[Q], w_scales[Q], w_grouped[Q])
+        regroup_h(0, nc.vector.tensor_copy)
+        add_pos(2, 1)
+        quantise_h(0)
+        spread_bias(bias_rows[0], q_add, Q_SCALE)
+        for j in range(3):
+            multiply(0, Q, j)
+        row_factors(1)
+        normalise(1, 0, nc.vector)
+        normalise(1, 1, nc.vector)
+        normalise(1, 2, nc.scalar)
+        normalise(1, 3, nc.scalar)
+        for j in range(ROW_TILES):
+            evacuate(0, Q, j)
+            if j == 0:
+                multiply(0, Q, 3)
+        store(0, Q)
+        for t in range(PACK - 1):
+            transpose(1, t)
+        weight(V, nc.scalar.copy)
+        spread_bias(bias_rows[1], v_add, 1.0)
+        add_pos(2, 2)
+        add_pos(2, 3)
+        row_mean(2)
+        quantise(w_codes[V], w_scales[V], w_grouped[V])
+        weight(K, nc.vector.tensor_copy)
+        for j in range(ROW_TILES):
+            square_dev(2, j)
+        row_std(2)
+        quantise(w_codes[K], w_scales[K], w_grouped[K])
+
+        done = 12
+        for step in range(B):
+            quantised, normal = live(step + 1), live(step + 2)
+            rows = range(done, min(B * ROW_TILES, done + ROW_TILES))
+            done += len(rows)
+            if step > 0:
+                multiply(step, Q, 0)
+                multiply(step, Q, 1)
+                multiply(step, Q, 2)
+            if quantised:
+                gain_bias(step + 1, 0)
+                transpose(step + 1, 3)
+                for t in range(1, PACK):
+                    gain_bias(step + 1, t)
+                regroup_h(step + 1, gpsimd_copy)
+            multiply(step, K, 0)
+            multiply(step, K, 1)
+            if normal:
+                row_factors(step + 2)
+                normalise(step + 2, 0, nc.vector)
+                normalise(step + 2, 1, nc.gpsimd)
+                normalise(step + 2, 2, nc.gpsimd)
+                normalise(step + 2, 3, nc.scalar)
+            for r in rows:
+                add_pos(r // ROW_TILES, r % ROW_TILES)
+            evacuate(step, K, 0)
+            evacuate(step, K, 1)
+            for r in rows:
+                square_dev(r // ROW_TILES, r % ROW_TILES)
+                if r % ROW_TILES == 3:
+                    row_std(r // ROW_TILES)
+            if step > 0:
+                evacuate(step, Q, 0)
+                multiply(step, Q, 3)
+                evacuate(step, Q, 1)
+                multiply(step, V, 0)
+                evacuate(step, Q, 2)
+                multiply(step, V, 1)
+                evacuate(step, Q, 3)
+                store(step, Q)
+                multiply(step, V, 2)
+            else:
+                multiply(step, V, 0)
+                multiply(step, V, 1)
+                multiply(step, V, 2)
+            multiply(step, K, 2)
+            evacuate(step, V, 0)
+            multiply(step, V, 3)
+            evacuate(step, V, 1)
+            multiply(step, K, 3)
+            evacuate(step, V, 2)
+            evacuate(step, K, 2)
+            evacuate(step, V, 3)
+            store(step, V)
+            evacuate(step, K, 3)
+            store(step, K)
+            if normal:
+                for t in range(PACK - 1):
+                    transpose(step + 2, t)
+            if quantised:
                 quantise_h(step + 1)
-            if live(step + 2):
-                gain_bias(step + 2, 1)
-            if live(step):
-                project(step, V, 0, o_sb[V])
-                project(step, V, 1, o_sb[V])
-                project(step, K, 2, o_sb[K])
-            if live(step + 3):
-                row_factors(step + 3)
-            if live(step + 2):
-                transpose(step + 2, 3)
-                gain_bias(step + 2, 2)
-            if live(step):
-                project(step, V, 2, o_sb[V])
-                project(step, V, 3, o_sb[V])
-                project(step, K, 3, o_sb[K])
-            if live(step + 2):
-                gain_bias(step + 2, 3)
-            if live(step):
-                store(step, o_sb[K], out_1)
-                store(step, o_sb[V], out_2)
+            for r in rows:
+                if r % ROW_TILES == 3:
+                    row_mean(r // ROW_TILES)

@@ -39,7 +39,7 @@ def tile_disentangledattention_pa_t_kernel(
         psum_qv = ctx.enter_context(tc.psum_pool(name="psum_qv", bufs=3))
         psum_k = ctx.enter_context(tc.psum_pool(name="psum_k", bufs=2))
 
-        x_sb, u, total, square, std, neg_mean, rstd, neg_shift = {}, {}, {}, {}, {}, {}, {}, {}
+        x_sb, u, total, square, neg_mean, rstd, neg_shift = {}, {}, {}, {}, {}, {}, {}
         z, z_t, h_t, grouped, h_codes, h_scales, acc_of, o_sb = {}, {}, {}, {}, {}, {}, {}, {}
 
         def live(b):
@@ -80,24 +80,26 @@ def tile_disentangledattention_pa_t_kernel(
                 accum_out=square[b][:, j : j + 1],
             )
 
-        def row_std(b):
-            std[b] = small.tile([P, ROW_TILES], F32, name="std")
+        def row_rstd(b):
+            rstd[b] = small.tile([P, ROW_TILES], F32, name="rstd")
             nc.scalar.activation(
-                out=std[b][:], in_=square[b][:], func=ACT.Sqrt, bias=EPS, scale=1.0 / float(H) ** 3
+                out=rstd[b][:],
+                in_=square[b][:],
+                func=ACT.Abs_reciprocal_sqrt,
+                bias=EPS,
+                scale=1.0 / float(H) ** 3,
             )
 
         def row_mean(b):
             neg_mean[b] = small.tile([P, ROW_TILES], F32, name="neg_mean")
             nc.vector.tensor_scalar_mul(out=neg_mean[b][:], in0=total[b][:], scalar1=-1.0 / H)
 
-        def row_factors(b):
-            rstd[b] = small.tile([P, ROW_TILES], F32, name="rstd")
-            nc.vector.reciprocal(out=rstd[b][:], in_=std[b][:])
+        def row_shift(b):
             neg_shift[b] = small.tile([P, ROW_TILES], F32, name="neg_shift")
             nc.vector.tensor_tensor(out=neg_shift[b][:], in0=neg_mean[b][:], in1=rstd[b][:], op=ALU.mult)
 
         def normalise(b, j, engine):
-            if j == 0:
+            if b not in z:
                 z[b] = work.tile([P, ROW_TILES, PACK, P], F32, name="z", bufs=3)
             z_j = z[b][:, j, :, :].rearrange("p t (c i) -> p c t i", i=4)
             u_j = u[b][:, j, :].rearrange("p (c i t) -> p c t i", i=4, t=PACK)
@@ -146,6 +148,12 @@ def tile_disentangledattention_pa_t_kernel(
 
         def gpsimd_copy(out, in_):
             nc.gpsimd.tensor_scalar(out=out, in0=in_, scalar1=1.0, scalar2=0.0, op0=ALU.mult, op1=ALU.add)
+
+        def wait_for_read(b, i):
+            tick = small.tile([P, 1], F32, name="tick")
+            nc.gpsimd.tensor_scalar(
+                out=tick[:], in0=o_sb[b, i][:, 0, 0, 0:1], scalar1=1.0, scalar2=0.0, op0=ALU.mult, op1=ALU.add
+            )
 
         def regroup_h(b, copy):
             grouped[b] = work.tile([P, S, PACK], BF16, name="grouped", align_bytes=64)
@@ -237,7 +245,7 @@ def tile_disentangledattention_pa_t_kernel(
         one = const.tile([P, 1], F32)
         nc.gpsimd.memset(one[:], 1.0)
         warm = const.tile([P, 1], F32)
-        nc.scalar.activation(out=warm[:], in_=one[:], func=ACT.Sqrt)
+        nc.scalar.activation(out=warm[:], in_=one[:], func=ACT.Abs_reciprocal_sqrt)
         gain = const.tile([P, PACK], F32)
         shift = const.tile([P, PACK], F32)
         q_add = const.tile([P, NH, HD], F32)
@@ -259,13 +267,13 @@ def tile_disentangledattention_pa_t_kernel(
 
         for j in range(ROW_TILES):
             sums(0, j)
-        row_std(0)
-        row_mean(0)
+        row_rstd(0)
         add_pos(1, 0)
+        row_mean(0)
         add_pos(1, 1)
+        row_shift(0)
         nc.vector.tensor_copy(out=gain[:], in_=gain_raw[:])
         nc.vector.tensor_copy(out=shift[:], in_=shift_raw[:])
-        row_factors(0)
         for j in range(ROW_TILES):
             normalise(0, j, nc.vector if j < 2 else nc.scalar)
         for t in range(PACK):
@@ -273,11 +281,11 @@ def tile_disentangledattention_pa_t_kernel(
             gain_bias(0, t)
         add_pos(1, 2)
         add_pos(1, 3)
-        row_mean(1)
         weight(Q, nc.vector.tensor_copy)
+        row_mean(1)
         for j in range(ROW_TILES):
             square_dev(1, j)
-        row_std(1)
+        row_rstd(1)
         add_pos(2, 0)
         quantise(w_codes[Q], w_scales[Q], w_grouped[Q])
         regroup_h(0, nc.vector.tensor_copy)
@@ -286,7 +294,7 @@ def tile_disentangledattention_pa_t_kernel(
         spread_bias(bias_rows[0], q_add, Q_SCALE)
         for j in range(3):
             multiply(0, Q, j)
-        row_factors(1)
+        row_shift(1)
         normalise(1, 0, nc.vector)
         normalise(1, 1, nc.vector)
         normalise(1, 2, nc.scalar)
@@ -302,12 +310,12 @@ def tile_disentangledattention_pa_t_kernel(
         spread_bias(bias_rows[1], v_add, 1.0)
         add_pos(2, 2)
         add_pos(2, 3)
-        row_mean(2)
         quantise(w_codes[V], w_scales[V], w_grouped[V])
+        row_mean(2)
         weight(K, nc.vector.tensor_copy)
         for j in range(ROW_TILES):
             square_dev(2, j)
-        row_std(2)
+        row_rstd(2)
         quantise(w_codes[K], w_scales[K], w_grouped[K])
 
         done = 12
@@ -324,14 +332,12 @@ def tile_disentangledattention_pa_t_kernel(
                 transpose(step + 1, 3)
                 for t in range(1, PACK):
                     gain_bias(step + 1, t)
-                regroup_h(step + 1, gpsimd_copy)
             multiply(step, K, 0)
             multiply(step, K, 1)
             if normal:
-                row_factors(step + 2)
                 normalise(step + 2, 0, nc.vector)
-                normalise(step + 2, 1, nc.gpsimd)
-                normalise(step + 2, 2, nc.gpsimd)
+                row_shift(step + 2)
+                normalise(step + 2, 1, nc.vector)
                 normalise(step + 2, 3, nc.scalar)
             for r in rows:
                 add_pos(r // ROW_TILES, r % ROW_TILES)
@@ -340,10 +346,15 @@ def tile_disentangledattention_pa_t_kernel(
             for r in rows:
                 square_dev(r // ROW_TILES, r % ROW_TILES)
                 if r % ROW_TILES == 3:
-                    row_std(r // ROW_TILES)
+                    row_rstd(r // ROW_TILES)
             if step > 0:
                 evacuate(step, Q, 0)
                 multiply(step, Q, 3)
+                if quantised:
+                    wait_for_read(step, Q)
+                    regroup_h(step + 1, gpsimd_copy)
+                if normal:
+                    normalise(step + 2, 2, nc.gpsimd)
                 evacuate(step, Q, 1)
                 multiply(step, V, 0)
                 evacuate(step, Q, 2)
@@ -357,6 +368,10 @@ def tile_disentangledattention_pa_t_kernel(
                 multiply(step, V, 2)
             multiply(step, K, 2)
             evacuate(step, V, 0)
+            if step == 0:
+                wait_for_read(step, V)
+                regroup_h(step + 1, gpsimd_copy)
+                normalise(step + 2, 2, nc.gpsimd)
             multiply(step, V, 3)
             evacuate(step, V, 1)
             multiply(step, K, 3)
@@ -369,8 +384,8 @@ def tile_disentangledattention_pa_t_kernel(
             if normal:
                 for t in range(PACK - 1):
                     transpose(step + 2, t)
-            if quantised:
-                quantise_h(step + 1)
             for r in rows:
                 if r % ROW_TILES == 3:
                     row_mean(r // ROW_TILES)
+            if quantised:
+                quantise_h(step + 1)

@@ -338,6 +338,7 @@ def tile_disentangledattention_pa_t_kernel(
                 normalise(step + 2, 0, nc.vector)
                 row_shift(step + 2)
                 normalise(step + 2, 1, nc.vector)
+                normalise(step + 2, 2, nc.vector)
                 normalise(step + 2, 3, nc.scalar)
             for r in rows:
                 add_pos(r // ROW_TILES, r % ROW_TILES)
@@ -353,8 +354,6 @@ def tile_disentangledattention_pa_t_kernel(
                 if quantised:
                     wait_for_read(step, Q)
                     regroup_h(step + 1, gpsimd_copy)
-                if normal:
-                    normalise(step + 2, 2, nc.gpsimd)
                 evacuate(step, Q, 1)
                 multiply(step, V, 0)
                 evacuate(step, Q, 2)
@@ -371,7 +370,6 @@ def tile_disentangledattention_pa_t_kernel(
             if step == 0:
                 wait_for_read(step, V)
                 regroup_h(step + 1, gpsimd_copy)
-                normalise(step + 2, 2, nc.gpsimd)
             multiply(step, V, 3)
             evacuate(step, V, 1)
             multiply(step, K, 3)

@@ -37,9 +37,9 @@ def tile_disentangledattention_pa_t_kernel(
         outs = ctx.enter_context(tc.tile_pool(name="outs", bufs=3))
         psum_t = ctx.enter_context(tc.psum_pool(name="psum_t", bufs=3))
         psum_qv = ctx.enter_context(tc.psum_pool(name="psum_qv", bufs=3))
-        psum_k = ctx.enter_context(tc.psum_pool(name="psum_k", bufs=2))
+        psum_xk = ctx.enter_context(tc.psum_pool(name="psum_xk", bufs=2))
 
-        x_sb, u, total, square, neg_mean, rstd, neg_shift = {}, {}, {}, {}, {}, {}, {}
+        x_sb, x_ps, u, total, square, neg_mean, rstd, neg_shift = {}, {}, {}, {}, {}, {}, {}, {}
         z, z_t, h_t, grouped, h_codes, h_scales, acc_of, o_sb = {}, {}, {}, {}, {}, {}, {}, {}
 
         def live(b):
@@ -53,13 +53,17 @@ def tile_disentangledattention_pa_t_kernel(
         def new_x(b):
             x_sb[b] = xs.tile([P, ROW_TILES, H], BF16, name="x_b")
 
+        def spread_x(b, j):
+            x_ps[b, j] = psum_xk.tile([P, H], F32, name="acc_xk")
+            nc.tensor.matmul(x_ps[b, j][:], lhsT=ident_bf16[:], rhs=x_sb[b][:, j, :], start=True, stop=True)
+
         def add_pos(b, j):
             if j == 0:
                 u[b] = work.tile([P, ROW_TILES, H], F32, name="u", bufs=5)
                 total[b] = small.tile([P, ROW_TILES], F32, name="total")
             nc.vector.scalar_tensor_tensor(
                 out=u[b][:, j, :],
-                in0=x_sb[b][:, j, :],
+                in0=x_ps[b, j][:],
                 scalar=1.0,
                 in1=pos_sb[:, j, :],
                 op0=ALU.mult,
@@ -149,12 +153,6 @@ def tile_disentangledattention_pa_t_kernel(
         def gpsimd_copy(out, in_):
             nc.gpsimd.tensor_scalar(out=out, in0=in_, scalar1=1.0, scalar2=0.0, op0=ALU.mult, op1=ALU.add)
 
-        def wait_for_read(b, i):
-            tick = small.tile([P, 1], F32, name="tick")
-            nc.gpsimd.tensor_scalar(
-                out=tick[:], in0=o_sb[b, i][:, 0, 0, 0:1], scalar1=1.0, scalar2=0.0, op0=ALU.mult, op1=ALU.add
-            )
-
         def regroup_h(b, copy):
             grouped[b] = work.tile([P, S, PACK], BF16, name="grouped", align_bytes=64)
             regroup(copy, grouped[b][:], h_t[b][:])
@@ -174,7 +172,7 @@ def tile_disentangledattention_pa_t_kernel(
                 o_sb[b, i] = outs.tile([P, NH, ROW_TILES, HD], F32, name="o%d" % i)
             rows = slice(j * P, (j + 1) * P)
             if i == K:
-                acc = psum_k.tile([P, H], F32, name="acc_k")
+                acc = psum_xk.tile([P, H], F32, name="acc_xk")
             else:
                 acc = psum_qv.tile([P, H], F32, name="acc_qv")
             nc.tensor.matmul_mx(
@@ -214,9 +212,9 @@ def tile_disentangledattention_pa_t_kernel(
         new_x(1)
         load_rows(x_sb[1], x[1], 0, ROW_TILES)
         gain_raw = const.tile([P, PACK], BF16)
-        nc.sync.dma_start(out=gain_raw[:], in_=emb_ln_g.rearrange("(p t) -> p t", t=PACK))
+        nc.scalar.dma_start(out=gain_raw[:], in_=emb_ln_g.rearrange("(p t) -> p t", t=PACK))
         shift_raw = const.tile([P, PACK], BF16)
-        nc.sync.dma_start(out=shift_raw[:], in_=emb_ln_b.rearrange("(p t) -> p t", t=PACK))
+        nc.scalar.dma_start(out=shift_raw[:], in_=emb_ln_b.rearrange("(p t) -> p t", t=PACK))
         w_raw, w_grouped, w_codes, w_scales = [], [], [], []
         for i, w in enumerate((Wq, Wk, Wv)):
             raw = const.tile([P, PACK, H], BF16, name="w_raw%d" % i)
@@ -240,6 +238,8 @@ def tile_disentangledattention_pa_t_kernel(
 
         ident = const.tile([P, P], F32)
         make_identity(nc, ident[:])
+        ident_bf16 = const.tile([P, P], BF16)
+        make_identity(nc, ident_bf16[:])
         ones = const.tile([P, P], BF16)
         nc.gpsimd.memset(ones[:], 1.0)
         one = const.tile([P, 1], F32)
@@ -247,12 +247,14 @@ def tile_disentangledattention_pa_t_kernel(
         warm = const.tile([P, 1], F32)
         nc.scalar.activation(out=warm[:], in_=one[:], func=ACT.Abs_reciprocal_sqrt)
         gain = const.tile([P, PACK], F32)
+        nc.gpsimd.tensor_copy(out=gain[:], in_=gain_raw[:])
         shift = const.tile([P, PACK], F32)
+        nc.gpsimd.tensor_copy(out=shift[:], in_=shift_raw[:])
         q_add = const.tile([P, NH, HD], F32)
         v_add = const.tile([P, NH, HD], F32)
 
         def spread_bias(row, dst, scale):
-            bank = psum_k.tile([P, H], F32, name="acc_k")
+            bank = psum_xk.tile([P, H], F32, name="acc_xk")
             nc.tensor.matmul(bank[:], lhsT=ones[:], rhs=row[:], start=True, stop=True)
             nc.scalar.activation(
                 out=dst[:].rearrange("p n d -> p (n d)"), in_=bank[:], func=ACT.Copy, scale=scale
@@ -262,98 +264,98 @@ def tile_disentangledattention_pa_t_kernel(
             regroup(copy, w_grouped[i][:], w_raw[i][:])
 
         def sums(b, j):
+            spread_x(b, j)
             add_pos(b, j)
-            square_dev(b, j)
 
         for j in range(ROW_TILES):
             sums(0, j)
+            square_dev(0, j)
         row_rstd(0)
-        add_pos(1, 0)
+        sums(1, 0)
         row_mean(0)
-        add_pos(1, 1)
-        row_shift(0)
-        nc.vector.tensor_copy(out=gain[:], in_=gain_raw[:])
-        nc.vector.tensor_copy(out=shift[:], in_=shift_raw[:])
+        sums(1, 1)
         for j in range(ROW_TILES):
-            normalise(0, j, nc.vector if j < 2 else nc.scalar)
-        for t in range(PACK):
+            normalise(0, j, nc.vector)
+        sums(1, 2)
+        sums(1, 3)
+        for t in (0, 1):
             transpose(0, t)
-            gain_bias(0, t)
-        add_pos(1, 2)
-        add_pos(1, 3)
+        gain_bias(0, 0)
+        transpose(0, 2)
+        gain_bias(0, 1)
+        transpose(0, 3)
+        gain_bias(0, 2)
+        gain_bias(0, 3)
         weight(Q, nc.vector.tensor_copy)
         row_mean(1)
         for j in range(ROW_TILES):
             square_dev(1, j)
         row_rstd(1)
-        add_pos(2, 0)
+        sums(2, 0)
         quantise(w_codes[Q], w_scales[Q], w_grouped[Q])
         regroup_h(0, nc.vector.tensor_copy)
-        add_pos(2, 1)
+        sums(2, 1)
         quantise_h(0)
         spread_bias(bias_rows[0], q_add, Q_SCALE)
         for j in range(3):
             multiply(0, Q, j)
-        row_shift(1)
-        normalise(1, 0, nc.vector)
-        normalise(1, 1, nc.vector)
-        normalise(1, 2, nc.scalar)
-        normalise(1, 3, nc.scalar)
         for j in range(ROW_TILES):
+            normalise(1, j, nc.gpsimd if j >= 2 else nc.vector)
+        evacuate(0, Q, 0)
+        multiply(0, Q, 3)
+        for j in range(1, ROW_TILES):
             evacuate(0, Q, j)
-            if j == 0:
-                multiply(0, Q, 3)
         store(0, Q)
-        for t in range(PACK - 1):
+        for t in range(3):
             transpose(1, t)
         weight(V, nc.scalar.copy)
         spread_bias(bias_rows[1], v_add, 1.0)
-        add_pos(2, 2)
-        add_pos(2, 3)
+        sums(2, 2)
+        sums(2, 3)
         quantise(w_codes[V], w_scales[V], w_grouped[V])
-        row_mean(2)
         weight(K, nc.vector.tensor_copy)
         for j in range(ROW_TILES):
             square_dev(2, j)
         row_rstd(2)
         quantise(w_codes[K], w_scales[K], w_grouped[K])
+        row_mean(2)
 
-        done = 12
         for step in range(B):
-            quantised, normal = live(step + 1), live(step + 2)
-            rows = range(done, min(B * ROW_TILES, done + ROW_TILES))
-            done += len(rows)
-            if step > 0:
-                multiply(step, Q, 0)
-                multiply(step, Q, 1)
-                multiply(step, Q, 2)
+            quantised, normal, more = live(step + 1), live(step + 2), live(step + 3)
+            if more:
+                for j in range(3):
+                    sums(step + 3, j)
+            elif step > 0:
+                for j in range(3):
+                    multiply(step, Q, j)
             if quantised:
                 gain_bias(step + 1, 0)
                 transpose(step + 1, 3)
-                for t in range(1, PACK):
-                    gain_bias(step + 1, t)
-            multiply(step, K, 0)
-            multiply(step, K, 1)
+            if more:
+                sums(step + 3, 3)
+            if quantised:
+                gain_bias(step + 1, 1)
+                gain_bias(step + 1, 2)
+                gain_bias(step + 1, 3)
+            if more and step > 0:
+                for j in range(3):
+                    multiply(step, Q, j)
             if normal:
-                normalise(step + 2, 0, nc.vector)
-                row_shift(step + 2)
-                normalise(step + 2, 1, nc.vector)
-                normalise(step + 2, 2, nc.vector)
-                normalise(step + 2, 3, nc.scalar)
-            for r in rows:
-                add_pos(r // ROW_TILES, r % ROW_TILES)
-            evacuate(step, K, 0)
-            evacuate(step, K, 1)
-            for r in rows:
-                square_dev(r // ROW_TILES, r % ROW_TILES)
-                if r % ROW_TILES == 3:
-                    row_rstd(r // ROW_TILES)
+                for j in range(ROW_TILES):
+                    normalise(step + 2, j, nc.gpsimd)
+            if quantised:
+                regroup_h(step + 1, gpsimd_copy)
+            if step == 0:
+                for j in range(3):
+                    multiply(step, V, j)
+            for j in range(3):
+                multiply(step, K, j)
+                evacuate(step, K, j)
+                if more:
+                    square_dev(step + 3, j)
             if step > 0:
                 evacuate(step, Q, 0)
                 multiply(step, Q, 3)
-                if quantised:
-                    wait_for_read(step, Q)
-                    regroup_h(step + 1, gpsimd_copy)
                 evacuate(step, Q, 1)
                 multiply(step, V, 0)
                 evacuate(step, Q, 2)
@@ -361,29 +363,21 @@ def tile_disentangledattention_pa_t_kernel(
                 evacuate(step, Q, 3)
                 store(step, Q)
                 multiply(step, V, 2)
-            else:
-                multiply(step, V, 0)
-                multiply(step, V, 1)
-                multiply(step, V, 2)
-            multiply(step, K, 2)
-            evacuate(step, V, 0)
-            if step == 0:
-                wait_for_read(step, V)
-                regroup_h(step + 1, gpsimd_copy)
-            multiply(step, V, 3)
-            evacuate(step, V, 1)
             multiply(step, K, 3)
-            evacuate(step, V, 2)
-            evacuate(step, K, 2)
-            evacuate(step, V, 3)
-            store(step, V)
             evacuate(step, K, 3)
             store(step, K)
+            if more:
+                square_dev(step + 3, 3)
+                row_rstd(step + 3)
+            evacuate(step, V, 0)
+            multiply(step, V, 3)
+            for j in range(1, ROW_TILES):
+                evacuate(step, V, j)
+            store(step, V)
             if normal:
-                for t in range(PACK - 1):
+                for t in range(3):
                     transpose(step + 2, t)
-            for r in rows:
-                if r % ROW_TILES == 3:
-                    row_mean(r // ROW_TILES)
             if quantised:
                 quantise_h(step + 1)
+            if more:
+                row_mean(step + 3)

@@ -153,6 +153,12 @@ def tile_disentangledattention_pa_t_kernel(
         def gpsimd_copy(out, in_):
             nc.gpsimd.tensor_scalar(out=out, in0=in_, scalar1=1.0, scalar2=0.0, op0=ALU.mult, op1=ALU.add)
 
+        def wait_for_read(b, i):
+            tick = small.tile([P, 1], F32, name="tick")
+            nc.gpsimd.tensor_scalar(
+                out=tick[:], in0=o_sb[b, i][:, 0, 0, 0:1], scalar1=1.0, scalar2=0.0, op0=ALU.mult, op1=ALU.add
+            )
+
         def regroup_h(b, copy):
             grouped[b] = work.tile([P, S, PACK], BF16, name="grouped", align_bytes=64)
             regroup(copy, grouped[b][:], h_t[b][:])
@@ -263,112 +269,160 @@ def tile_disentangledattention_pa_t_kernel(
         def weight(i, copy):
             regroup(copy, w_grouped[i][:], w_raw[i][:])
 
-        def sums(b, j):
-            spread_x(b, j)
-            add_pos(b, j)
-
         for j in range(ROW_TILES):
-            sums(0, j)
+            spread_x(0, j)
+            add_pos(0, j)
             square_dev(0, j)
         row_rstd(0)
-        sums(1, 0)
+        weight(Q, nc.scalar.copy)
+        spread_x(1, 0)
+        add_pos(1, 0)
         row_mean(0)
-        sums(1, 1)
+        spread_x(1, 1)
+        add_pos(1, 1)
+        spread_x(1, 2)
+        spread_x(1, 3)
         for j in range(ROW_TILES):
             normalise(0, j, nc.vector)
-        sums(1, 2)
-        sums(1, 3)
-        for t in (0, 1):
+        for t in range(3):
             transpose(0, t)
         gain_bias(0, 0)
-        transpose(0, 2)
-        gain_bias(0, 1)
         transpose(0, 3)
-        gain_bias(0, 2)
-        gain_bias(0, 3)
-        weight(Q, nc.vector.tensor_copy)
-        row_mean(1)
+        for t in range(1, PACK):
+            gain_bias(0, t)
+        add_pos(1, 2)
+        add_pos(1, 3)
         for j in range(ROW_TILES):
             square_dev(1, j)
         row_rstd(1)
-        sums(2, 0)
+        spread_x(2, 0)
+        spread_x(2, 1)
         quantise(w_codes[Q], w_scales[Q], w_grouped[Q])
-        regroup_h(0, nc.vector.tensor_copy)
-        sums(2, 1)
-        quantise_h(0)
+        add_pos(2, 0)
+        add_pos(2, 1)
         spread_bias(bias_rows[0], q_add, Q_SCALE)
+        spread_x(2, 2)
+        regroup_h(0, nc.vector.tensor_copy)
+        row_mean(1)
+        add_pos(2, 2)
+        quantise_h(0)
         for j in range(3):
             multiply(0, Q, j)
         for j in range(ROW_TILES):
-            normalise(1, j, nc.gpsimd if j >= 2 else nc.vector)
+            normalise(1, j, nc.vector)
+        for t in range(3):
+            transpose(1, t)
+        gain_bias(1, 0)
         evacuate(0, Q, 0)
         multiply(0, Q, 3)
+        transpose(1, 3)
+        for t in range(1, PACK):
+            gain_bias(1, t)
+        wait_for_read(0, Q)
+        weight(V, gpsimd_copy)
         for j in range(1, ROW_TILES):
             evacuate(0, Q, j)
         store(0, Q)
-        for t in range(3):
-            transpose(1, t)
-        weight(V, nc.scalar.copy)
+        spread_x(2, 3)
+        add_pos(2, 3)
         spread_bias(bias_rows[1], v_add, 1.0)
-        sums(2, 2)
-        sums(2, 3)
-        quantise(w_codes[V], w_scales[V], w_grouped[V])
         weight(K, nc.vector.tensor_copy)
         for j in range(ROW_TILES):
             square_dev(2, j)
         row_rstd(2)
+        quantise(w_codes[V], w_scales[V], w_grouped[V])
         quantise(w_codes[K], w_scales[K], w_grouped[K])
-        row_mean(2)
+        for j in range(3):
+            multiply(0, V, j)
+        multiply(0, K, 0)
+        multiply(0, K, 1)
+        evacuate(0, V, 0)
+        wait_for_read(0, V)
+        regroup_h(1, gpsimd_copy)
+        multiply(0, V, 3)
+        for j in range(1, ROW_TILES):
+            evacuate(0, V, j)
+        store(0, V)
+        evacuate(0, K, 0)
+        spread_x(3, 0)
+        evacuate(0, K, 1)
+        spread_x(3, 1)
+        for j in range(ROW_TILES):
+            add_pos(3, j)
+            if j == 0:
+                multiply(0, K, 2)
+                evacuate(0, K, 2)
+            if j == 1:
+                multiply(0, K, 3)
+                evacuate(0, K, 3)
+                store(0, K)
+                spread_x(3, 2)
+                spread_x(3, 3)
+                row_mean(2)
+                quantise_h(1)
+                for i in range(ROW_TILES):
+                    normalise(2, i, nc.vector)
+        for j in range(ROW_TILES):
+            square_dev(3, j)
+        row_rstd(3)
+        row_mean(3)
+        for t in range(3):
+            transpose(2, t)
+        spread_x(4, 0)
+        spread_x(4, 1)
 
-        for step in range(B):
-            quantised, normal, more = live(step + 1), live(step + 2), live(step + 3)
-            if more:
-                for j in range(3):
-                    sums(step + 3, j)
-            elif step > 0:
+        for step in range(1, B):
+            quantised, normal, sums = live(step + 1), live(step + 2), live(step + 3)
+            if sums:
+                add_pos(step + 3, 0)
+                add_pos(step + 3, 1)
+            else:
                 for j in range(3):
                     multiply(step, Q, j)
+            if sums:
+                spread_x(step + 3, 2)
+                add_pos(step + 3, 2)
             if quantised:
                 gain_bias(step + 1, 0)
                 transpose(step + 1, 3)
-            if more:
-                sums(step + 3, 3)
-            if quantised:
-                gain_bias(step + 1, 1)
-                gain_bias(step + 1, 2)
-                gain_bias(step + 1, 3)
-            if more and step > 0:
+                for t in range(1, PACK):
+                    gain_bias(step + 1, t)
+            if sums:
+                spread_x(step + 3, 3)
+                add_pos(step + 3, 3)
                 for j in range(3):
                     multiply(step, Q, j)
+                square_dev(step + 3, 0)
             if normal:
                 for j in range(ROW_TILES):
                     normalise(step + 2, j, nc.gpsimd)
             if quantised:
                 regroup_h(step + 1, gpsimd_copy)
-            if step == 0:
-                for j in range(3):
-                    multiply(step, V, j)
-            for j in range(3):
-                multiply(step, K, j)
-                evacuate(step, K, j)
-                if more:
-                    square_dev(step + 3, j)
-            if step > 0:
-                evacuate(step, Q, 0)
-                multiply(step, Q, 3)
-                evacuate(step, Q, 1)
-                multiply(step, V, 0)
-                evacuate(step, Q, 2)
-                multiply(step, V, 1)
-                evacuate(step, Q, 3)
-                store(step, Q)
-                multiply(step, V, 2)
+            multiply(step, K, 0)
+            multiply(step, K, 1)
+            evacuate(step, K, 0)
+            if sums:
+                square_dev(step + 3, 1)
+            evacuate(step, K, 1)
+            if sums:
+                square_dev(step + 3, 2)
+            evacuate(step, Q, 0)
+            multiply(step, Q, 3)
+            multiply(step, K, 2)
+            evacuate(step, Q, 1)
+            multiply(step, V, 0)
+            evacuate(step, Q, 2)
+            multiply(step, V, 1)
+            evacuate(step, Q, 3)
+            store(step, Q)
             multiply(step, K, 3)
-            evacuate(step, K, 3)
-            store(step, K)
-            if more:
+            multiply(step, V, 2)
+            evacuate(step, K, 2)
+            if sums:
                 square_dev(step + 3, 3)
                 row_rstd(step + 3)
+            evacuate(step, K, 3)
+            store(step, K)
             evacuate(step, V, 0)
             multiply(step, V, 3)
             for j in range(1, ROW_TILES):
@@ -377,7 +431,10 @@ def tile_disentangledattention_pa_t_kernel(
             if normal:
                 for t in range(3):
                     transpose(step + 2, t)
+            if live(step + 4):
+                spread_x(step + 4, 0)
+                spread_x(step + 4, 1)
             if quantised:
                 quantise_h(step + 1)
-            if more:
+            if sums:
                 row_mean(step + 3)

@@ -205,7 +205,8 @@ def tile_disentangledattention_pa_t_kernel(
                 nc.vector.tensor_tensor(out=o_j, in0=by_head, in1=v_add[:], op=ALU.add)
 
         def store(b, i):
-            nc.sync.dma_start(
+            queue = nc.scalar if i == K else nc.sync
+            queue.dma_start(
                 out=(out_0, out_1, out_2)[i][b].rearrange("n (p j) d -> p n (j d)", j=ROW_TILES),
                 in_=o_sb[b, i][:].rearrange("p n j d -> p n (j d)"),
             )

from contextlib import ExitStack
import math

import concourse.mybir as mybir
from concourse.masks import make_identity

F32 = mybir.dt.float32
BF16 = mybir.dt.bfloat16
U32 = mybir.dt.uint32
U8 = mybir.dt.uint8
FP8X4 = mybir.dt.float8_e4m3fn_x4
ALU = mybir.AluOpType
ACT = mybir.ActivationFunctionType

P = 128
PACK = 4
B, S, H, NH, HD = 8, 512, 512, 4, 128
ROW_TILES = S // P
EPS = 1e-7
Q_SCALE = 1.0 / math.sqrt(HD)

Q, K, V = 0, 1, 2

FLOPS = 2 * B * S * H * 3 * H


def tile_disentangledattention_pa_t_kernel(
    tc, x, pos_emb, emb_ln_g, emb_ln_b, Wq, Wk, Wv, q_bias, v_bias, out_0, out_1, out_2
):
    nc = tc.nc
    with ExitStack() as ctx:
        ctx.enter_context(tc.manual_schedule())
        const = ctx.enter_context(tc.tile_pool(name="const", bufs=1))
        xs = ctx.enter_context(tc.tile_pool(name="xs", bufs=6))
        work = ctx.enter_context(tc.tile_pool(name="work", bufs=2))
        small = ctx.enter_context(tc.tile_pool(name="small", bufs=6))
        outs = ctx.enter_context(tc.tile_pool(name="outs", bufs=3))
        psum_t = ctx.enter_context(tc.psum_pool(name="psum_t", bufs=3))
        psum_qv = ctx.enter_context(tc.psum_pool(name="psum_qv", bufs=3))
        psum_xk = ctx.enter_context(tc.psum_pool(name="psum_xk", bufs=2))

        x_sb, x_ps, u, total, square, neg_mean, rstd, neg_shift = {}, {}, {}, {}, {}, {}, {}, {}
        z, z_t, h_t, grouped, h_codes, h_scales, acc_of, o_sb = {}, {}, {}, {}, {}, {}, {}, {}

        def live(b):
            return 0 <= b < B

        def load_rows(dst, src, j0, j1):
            nc.sync.dma_start(
                out=dst[:, j0:j1, :], in_=src.rearrange("(p j) h -> p j h", j=ROW_TILES)[:, j0:j1, :]
            )

        def new_x(b):
            x_sb[b] = xs.tile([P, ROW_TILES, H], BF16, name="x_b")

        def spread_x(b, j):
            x_ps[b, j] = psum_xk.tile([P, H], F32, name="acc_xk")
            nc.tensor.matmul(x_ps[b, j][:], lhsT=ident_bf16[:], rhs=x_sb[b][:, j, :], start=True, stop=True)

        def add_pos(b, j):
            if j == 0:
                u[b] = work.tile([P, ROW_TILES, H], F32, name="u", bufs=5)
                total[b] = small.tile([P, ROW_TILES], F32, name="total")
            nc.vector.scalar_tensor_tensor(
                out=u[b][:, j, :],
                in0=x_ps[b, j][:],
                scalar=1.0,
                in1=pos_sb[:, j, :],
                op0=ALU.mult,
                op1=ALU.add,
                accum_out=total[b][:, j : j + 1],
            )

        def square_dev(b, j):
            if j == 0:
                square[b] = small.tile([P, ROW_TILES], F32, name="square")
            dev = work.tile([P, H], BF16, name="dev")
            nc.scalar.activation(
                out=dev[:],
                in_=u[b][:, j, :],
                func=ACT.Square,
                scale=-float(H),
                bias=total[b][:, j : j + 1],
                accum_out=square[b][:, j : j + 1],
            )

        def row_rstd(b):
            rstd[b] = small.tile([P, ROW_TILES], F32, name="rstd")
            nc.scalar.activation(
                out=rstd[b][:],
                in_=square[b][:],
                func=ACT.Abs_reciprocal_sqrt,
                bias=EPS,
                scale=1.0 / float(H) ** 3,
            )

        def row_mean(b):
            neg_mean[b] = small.tile([P, ROW_TILES], F32, name="neg_mean")
            nc.vector.tensor_scalar_mul(out=neg_mean[b][:], in0=total[b][:], scalar1=-1.0 / H)

        def row_shift(b):
            neg_shift[b] = small.tile([P, ROW_TILES], F32, name="neg_shift")
            nc.vector.tensor_tensor(out=neg_shift[b][:], in0=neg_mean[b][:], in1=rstd[b][:], op=ALU.mult)

        def normalise(b, j, engine):
            if b not in z:
                z[b] = work.tile([P, ROW_TILES, PACK, P], F32, name="z", bufs=3)
            z_j = z[b][:, j, :, :].rearrange("p t (c i) -> p c t i", i=4)
            u_j = u[b][:, j, :].rearrange("p (c i t) -> p c t i", i=4, t=PACK)
            if engine is nc.scalar:
                nc.scalar.activation(
                    out=z_j,
                    in_=u_j,
                    func=ACT.Identity,
                    scale=rstd[b][:, j : j + 1],
                    bias=neg_shift[b][:, j : j + 1],
                )
            else:
                engine.tensor_scalar(
                    out=z_j,
                    in0=u_j,
                    scalar1=neg_mean[b][:, j : j + 1],
                    scalar2=rstd[b][:, j : j + 1],
                    op0=ALU.add,
                    op1=ALU.mult,
                )

        def transpose(b, t):
            z_t[b, t] = psum_t.tile([P, S], F32, name="z_t")
            for j in range(ROW_TILES):
                nc.tensor.transpose(z_t[b, t][:, j * P : (j + 1) * P], z[b][:, j, t, :], ident[:])

        def gain_bias(b, t):
            if t == 0:
                h_t[b] = work.tile([P, PACK, S], BF16, name="h_t")
            nc.scalar.activation(
                out=h_t[b][:, t, :],
                in_=z_t[b, t][:],
                func=ACT.Identity,
                scale=gain[:, t : t + 1],
                bias=shift[:, t : t + 1],
            )

        def regroup(copy, dst, src):
            if copy is gpsimd_copy:
                copy(out=dst, in_=src.rearrange("p t c -> p c t"))
                return
            copy(
                out=dst.rearrange("p (c i) t -> p c t i", i=4),
                in_=src.rearrange("p t (c i) -> p c t i", i=4),
            )

        def gpsimd_copy(out, in_):
            nc.gpsimd.tensor_scalar(out=out, in0=in_, scalar1=1.0, scalar2=0.0, op0=ALU.mult, op1=ALU.add)

        def wait_for_read(b, i):
            tick = small.tile([P, 1], F32, name="tick")
            nc.gpsimd.tensor_scalar(
                out=tick[:], in0=o_sb[b, i][:, 0, 0, 0:1], scalar1=1.0, scalar2=0.0, op0=ALU.mult, op1=ALU.add
            )

        def regroup_h(b, copy):
            grouped[b] = work.tile([P, S, PACK], BF16, name="grouped", align_bytes=64)
            regroup(copy, grouped[b][:], h_t[b][:])

        def quantise(codes, scales, src):
            nc.vector.quantize_mx(
                out=codes[:].bitcast(FP8X4), scales=scales[:], in_=src[:].rearrange("p r t -> p (r t)")
            )

        def quantise_h(b):
            h_codes[b] = work.tile([P, S], U32, name="h_codes", align_bytes=64)
            h_scales[b] = work.tile([P, S], U8, name="h_scales", align_bytes=64)
            quantise(h_codes[b], h_scales[b], grouped[b])

        def multiply(b, i, j):
            if j == 0:
                o_sb[b, i] = outs.tile([P, NH, ROW_TILES, HD], F32, name="o%d" % i)
            rows = slice(j * P, (j + 1) * P)
            if i == K:
                acc = psum_xk.tile([P, H], F32, name="acc_xk")
            else:
                acc = psum_qv.tile([P, H], F32, name="acc_qv")
            nc.tensor.matmul_mx(
                out=acc[:],
                lhsT=h_codes[b][:, rows].bitcast(FP8X4),
                lhsT_scale=h_scales[b][:, rows],
                rhs=w_codes[i][:].bitcast(FP8X4),
                rhs_scale=w_scales[i][:],
                start=True,
                stop=True,
            )
            acc_of[b, i, j] = acc

        def evacuate(b, i, j):
            by_head = acc_of[b, i, j][:].rearrange("p (n d) -> p n d", n=NH)
            o_j = o_sb[b, i][:, :, j, :]
            if i == Q:
                nc.vector.scalar_tensor_tensor(
                    out=o_j, in0=by_head, scalar=Q_SCALE, in1=q_add[:], op0=ALU.mult, op1=ALU.add
                )
            elif i == K:
                nc.scalar.copy(out=o_j, in_=by_head)
            else:
                nc.vector.tensor_tensor(out=o_j, in0=by_head, in1=v_add[:], op=ALU.add)

        def store(b, i):
            queue = nc.scalar if i == K else nc.sync
            queue.dma_start(
                out=(out_0, out_1, out_2)[i][b].rearrange("n (p j) d -> p n (j d)", j=ROW_TILES),
                in_=o_sb[b, i][:].rearrange("p n j d -> p n (j d)"),
            )

        pos_sb = const.tile([P, ROW_TILES, H], BF16)
        new_x(0)
        for j in (0, 2):
            load_rows(x_sb[0], x[0], j, j + 2)
            load_rows(pos_sb, pos_emb, j, j + 2)
        new_x(1)
        load_rows(x_sb[1], x[1], 0, ROW_TILES)
        gain_raw = const.tile([P, PACK], BF16)
        nc.scalar.dma_start(out=gain_raw[:], in_=emb_ln_g.rearrange("(p t) -> p t", t=PACK))
        shift_raw = const.tile([P, PACK], BF16)
        nc.scalar.dma_start(out=shift_raw[:], in_=emb_ln_b.rearrange("(p t) -> p t", t=PACK))
        w_raw, w_grouped, w_codes, w_scales = [], [], [], []
        for i, w in enumerate((Wq, Wk, Wv)):
            raw = const.tile([P, PACK, H], BF16, name="w_raw%d" % i)
            nc.sync.dma_start(out=raw[:], in_=w.rearrange("(p t) n -> p t n", t=PACK))
            w_raw.append(raw)
            g_w = const.tile([P, H, PACK], BF16, name="w_grouped%d" % i, align_bytes=64)
            w_grouped.append(g_w)
            codes = const.tile([P, H], U32, name="w_codes%d" % i, align_bytes=64)
            w_codes.append(codes)
            scales = const.tile([P, H], U8, name="w_scales%d" % i, align_bytes=64)
            w_scales.append(scales)
        bias_rows = []
        for i, bias in enumerate((q_bias, v_bias)):
            row = const.tile([P, H], BF16, name="bias_row%d" % i)
            nc.gpsimd.memset(row[:], 0.0)
            nc.sync.dma_start(out=row[0:1, :], in_=bias.unsqueeze(0))
            bias_rows.append(row)
        for b in range(2, B):
            new_x(b)
            load_rows(x_sb[b], x[b], 0, ROW_TILES)

        ident = const.tile([P, P], F32)
        make_identity(nc, ident[:])
        ident_bf16 = const.tile([P, P], BF16)
        make_identity(nc, ident_bf16[:])
        ones = const.tile([P, P], BF16)
        nc.gpsimd.memset(ones[:], 1.0)
        one = const.tile([P, 1], F32)
        nc.gpsimd.memset(one[:], 1.0)
        warm = const.tile([P, 1], F32)
        nc.scalar.activation(out=warm[:], in_=one[:], func=ACT.Abs_reciprocal_sqrt)
        gain = const.tile([P, PACK], F32)
        nc.gpsimd.tensor_copy(out=gain[:], in_=gain_raw[:])
        shift = const.tile([P, PACK], F32)
        nc.gpsimd.tensor_copy(out=shift[:], in_=shift_raw[:])
        q_add = const.tile([P, NH, HD], F32)
        v_add = const.tile([P, NH, HD], F32)

        def spread_bias(row, dst, scale):
            bank = psum_xk.tile([P, H], F32, name="acc_xk")
            nc.tensor.matmul(bank[:], lhsT=ones[:], rhs=row[:], start=True, stop=True)
            nc.scalar.activation(
                out=dst[:].rearrange("p n d -> p (n d)"), in_=bank[:], func=ACT.Copy, scale=scale
            )

        def weight(i, copy):
            regroup(copy, w_grouped[i][:], w_raw[i][:])

        for j in range(ROW_TILES):
            spread_x(0, j)
            add_pos(0, j)
            square_dev(0, j)
        row_rstd(0)
        weight(Q, nc.scalar.copy)
        spread_x(1, 0)
        add_pos(1, 0)
        row_mean(0)
        spread_x(1, 1)
        add_pos(1, 1)
        spread_x(1, 2)
        spread_x(1, 3)
        for j in range(ROW_TILES):
            normalise(0, j, nc.vector)
        for t in range(3):
            transpose(0, t)
        gain_bias(0, 0)
        transpose(0, 3)
        for t in range(1, PACK):
            gain_bias(0, t)
        add_pos(1, 2)
        add_pos(1, 3)
        for j in range(ROW_TILES):
            square_dev(1, j)
        row_rstd(1)
        spread_x(2, 0)
        spread_x(2, 1)
        quantise(w_codes[Q], w_scales[Q], w_grouped[Q])
        add_pos(2, 0)
        add_pos(2, 1)
        spread_bias(bias_rows[0], q_add, Q_SCALE)
        spread_x(2, 2)
        regroup_h(0, nc.vector.tensor_copy)
        row_mean(1)
        add_pos(2, 2)
        quantise_h(0)
        for j in range(3):
            multiply(0, Q, j)
        for j in range(ROW_TILES):
            normalise(1, j, nc.vector)
        for t in range(3):
            transpose(1, t)
        gain_bias(1, 0)
        evacuate(0, Q, 0)
        multiply(0, Q, 3)
        transpose(1, 3)
        for t in range(1, PACK):
            gain_bias(1, t)
        wait_for_read(0, Q)
        weight(V, gpsimd_copy)
        for j in range(1, ROW_TILES):
            evacuate(0, Q, j)
        store(0, Q)
        spread_x(2, 3)
        add_pos(2, 3)
        spread_bias(bias_rows[1], v_add, 1.0)
        weight(K, nc.vector.tensor_copy)
        for j in range(ROW_TILES):
            square_dev(2, j)
        row_rstd(2)
        quantise(w_codes[V], w_scales[V], w_grouped[V])
        quantise(w_codes[K], w_scales[K], w_grouped[K])
        for j in range(3):
            multiply(0, V, j)
        multiply(0, K, 0)
        multiply(0, K, 1)
        evacuate(0, V, 0)
        wait_for_read(0, V)
        regroup_h(1, gpsimd_copy)
        multiply(0, V, 3)
        for j in range(1, ROW_TILES):
            evacuate(0, V, j)
        store(0, V)
        evacuate(0, K, 0)
        spread_x(3, 0)
        evacuate(0, K, 1)
        spread_x(3, 1)
        for j in range(ROW_TILES):
            add_pos(3, j)
            if j == 0:
                multiply(0, K, 2)
                evacuate(0, K, 2)
            if j == 1:
                multiply(0, K, 3)
                evacuate(0, K, 3)
                store(0, K)
                spread_x(3, 2)
                spread_x(3, 3)
                row_mean(2)
                quantise_h(1)
                for i in range(ROW_TILES):
                    normalise(2, i, nc.vector)
        for j in range(ROW_TILES):
            square_dev(3, j)
        row_rstd(3)
        row_mean(3)
        for t in range(3):
            transpose(2, t)
        spread_x(4, 0)
        spread_x(4, 1)

        for step in range(1, B):
            quantised, normal, sums = live(step + 1), live(step + 2), live(step + 3)
            if sums:
                add_pos(step + 3, 0)
                add_pos(step + 3, 1)
            else:
                for j in range(3):
                    multiply(step, Q, j)
            if sums:
                spread_x(step + 3, 2)
                add_pos(step + 3, 2)
            if quantised:
                gain_bias(step + 1, 0)
                transpose(step + 1, 3)
                for t in range(1, PACK):
                    gain_bias(step + 1, t)
            if sums:
                spread_x(step + 3, 3)
                add_pos(step + 3, 3)
                for j in range(3):
                    multiply(step, Q, j)
                square_dev(step + 3, 0)
            if normal:
                for j in range(ROW_TILES):
                    normalise(step + 2, j, nc.gpsimd)
            if quantised:
                regroup_h(step + 1, gpsimd_copy)
            multiply(step, K, 0)
            multiply(step, K, 1)
            evacuate(step, K, 0)
            if sums:
                square_dev(step + 3, 1)
            evacuate(step, K, 1)
            if sums:
                square_dev(step + 3, 2)
            evacuate(step, Q, 0)
            multiply(step, Q, 3)
            multiply(step, K, 2)
            evacuate(step, Q, 1)
            multiply(step, V, 0)
            evacuate(step, Q, 2)
            multiply(step, V, 1)
            evacuate(step, Q, 3)
            store(step, Q)
            multiply(step, K, 3)
            multiply(step, V, 2)
            evacuate(step, K, 2)
            if sums:
                square_dev(step + 3, 3)
                row_rstd(step + 3)
            evacuate(step, K, 3)
            store(step, K)
            evacuate(step, V, 0)
            multiply(step, V, 3)
            for j in range(1, ROW_TILES):
                evacuate(step, V, j)
            store(step, V)
            if normal:
                for t in range(3):
                    transpose(step + 2, t)
            if live(step + 4):
                spread_x(step + 4, 0)
                spread_x(step + 4, 1)
            if quantised:
                quantise_h(step + 1)
            if sums:
                row_mean(step + 3)
